import numpy as np
import ml_dtypes

BF16 = ml_dtypes.bfloat16


def bf(x):
    return np.asarray(x, np.float32).astype(BF16)


def f32(x):
    return np.asarray(x, np.float32)


def f64(x):
    return np.asarray(x).astype(np.float64)


def striped(idx):
    return np.tile(idx.reshape(-1, 16).T, (8, 1))


D, S, CH, W, K, N = 256, 4096, 8, 1024, 512, 8192


def setup_inputs():
    return {"table": f32(np.random.standard_normal((D, S))), "latent": bf(0.4 * np.random.standard_normal((K, D))), "offs": striped(np.random.permutation(np.tile(np.arange(S), 2))[:N])}


def reference(table, latent, offs):
    idx = offs[:16].T.reshape(-1)
    lat = f64(latent)
    summed = f64(table)[:, idx].reshape(D, CH, W).sum(axis=1)
    lang = np.tanh(summed / CH)
    scores = lang.T @ lat.T
    e = np.exp(scores)
    dist = e / e.sum(axis=1, keepdims=True)
    return lang + (dist @ lat).T

@@ -1,0 +1,107 @@
+import concourse.mybir as mybir
+from concourse.masks import make_identity
+
+F32, BF16, U16 = mybir.dt.float32, mybir.dt.bfloat16, mybir.dt.uint16
+ADD = mybir.AluOpType.add
+ACT = mybir.ActivationFunctionType
+X = mybir.AxisListType.X
+
+P = 128
+D, S, T, W, K = 256, 4096, 8, 1024, 512
+DB = D // P
+KB = K // P
+PIECE = 512
+
+FLOPS = 4 * W * K * D
+
+
+def tile_sde_kernel(tc, table, latent, offs, out):
+    nc = tc.nc
+    with (
+        tc.tile_pool(name="held", bufs=1) as held,
+        tc.tile_pool(name="work", bufs=2) as work,
+        tc.tile_pool(name="stats", bufs=4) as stats,
+        tc.psum_pool(name="psum", bufs=2) as psum,
+    ):
+        offsets = held.tile([P, T * W // 16], U16, name="offsets")
+        nc.sync.dma_start(offsets[:], offs)
+        tables = [held.tile([P, S], F32, name=f"table{b}") for b in range(DB)]
+        for b in range(DB):
+            nc.sync.dma_start(tables[b][:], table[b * P : (b + 1) * P, :])
+        codes = held.tile([P, KB, D], BF16, name="codes")
+        nc.sync.dma_start(codes[:], latent.rearrange("(c p) d -> p c d", p=P))
+
+        ident_bf = held.tile([P, P], BF16, name="ident_bf")
+        make_identity(nc, ident_bf[:])
+        ident_f32 = held.tile([P, P], F32, name="ident_f32")
+        make_identity(nc, ident_f32[:])
+
+        codesT = [held.tile([P, K], BF16, name=f"codesT{b}") for b in range(DB)]
+        for b in range(DB):
+            flipped = psum.tile([P, K], BF16, name="flipped")
+            for c in range(KB):
+                nc.tensor.transpose(
+                    flipped[:, c * P : (c + 1) * P], codes[:, c, b * P : (b + 1) * P], ident_bf[:]
+                )
+            nc.scalar.copy(codesT[b][:], flipped[:])
+
+        partial = [[held.tile([P, W], F32, name=f"partial{b}_{i}") for i in range(2)] for b in range(DB)]
+        summed = [partial[b][(T - 1) % 2] for b in range(DB)]
+        lang = [held.tile([P, W], F32, name=f"lang{b}") for b in range(DB)]
+        lang_bf = [held.tile([P, W], BF16, name=f"lang_bf{b}") for b in range(DB)]
+        result = [held.tile([P, W], F32, name=f"result{b}") for b in range(DB)]
+
+        for first_word in range(0, W, PIECE):
+            piece = slice(first_word, first_word + PIECE)
+
+            for b in range(DB):
+                for t in range(T):
+                    first_col = (t * W + first_word) // 16
+                    picked = tables[b][:].indirect(offsets[:, first_col : first_col + PIECE // 16])
+                    if t == 0:
+                        nc.vector.tensor_copy(partial[b][0][:, piece], picked)
+                    else:
+                        nc.vector.tensor_tensor(
+                            partial[b][t % 2][:, piece], picked, partial[b][(t - 1) % 2][:, piece], ADD
+                        )
+                nc.scalar.activation(lang_bf[b][:, piece], summed[b][:, piece], ACT.Tanh, scale=1.0 / T)
+                nc.scalar.activation(lang[b][:, piece], summed[b][:, piece], ACT.Tanh, scale=1.0 / T)
+
+            for w in range(first_word, first_word + PIECE, P):
+                words = slice(w, w + P)
+                scores = psum.tile([P, K], F32, name="scores")
+                for b in range(DB):
+                    nc.tensor.matmul(
+                        scores[:], lang_bf[b][:, words], codesT[b][:], start=(b == 0), stop=(b == DB - 1)
+                    )
+                negmax = stats.tile([P, 1], F32, name="negmax")
+                nc.vector.reduce_max(negmax[:], scores[:], axis=X, negate=True)
+                weights = work.tile([P, K], BF16, name="weights")
+                total = stats.tile([P, 1], F32, name="total")
+                nc.scalar.activation(weights[:], scores[:], ACT.Exp, bias=negmax[:], accum_out=total[:])
+                inverse = stats.tile([P, 1], F32, name="inverse")
+                nc.vector.reciprocal(inverse[:], total[:])
+
+                flipped = psum.tile([P, K], BF16, name="flipped")
+                for c in range(KB):
+                    nc.tensor.transpose(
+                        flipped[:, c * P : (c + 1) * P], weights[:, c * P : (c + 1) * P], ident_bf[:]
+                    )
+                weightsT = work.tile([P, K], BF16, name="weightsT")
+                nc.scalar.copy(weightsT[:], flipped[:])
+                mix = psum.tile([P, D], F32, name="mix")
+                for c in range(KB):
+                    nc.tensor.matmul(
+                        mix[:], weightsT[:, c * P : (c + 1) * P], codes[:, c, :], start=(c == 0), stop=(c == KB - 1)
+                    )
+                divided = work.tile([P, D], F32, name="divided")
+                nc.scalar.activation(divided[:], mix[:], ACT.Copy, scale=inverse[:])
+
+                back = psum.tile([P, D], F32, name="back")
+                for b in range(DB):
+                    nc.tensor.transpose(back[:, b * P : (b + 1) * P], divided[:, b * P : (b + 1) * P], ident_f32[:])
+                for b in range(DB):
+                    nc.vector.tensor_tensor(result[b][:, words], back[:, b * P : (b + 1) * P], lang[b][:, words], ADD)
+
+            for b in range(DB):
+                nc.sync.dma_start(out[b * P : (b + 1) * P, piece], result[b][:, piece])

@@ -10,7 +10,8 @@ P = 128
 D, S, T, W, K = 256, 4096, 8, 1024, 512
 DB = D // P
 KB = K // P
-PIECE = 512
+PIECES = (256, 256, 256, 128, 128)
+assert sum(PIECES) == W
 
 FLOPS = 4 * W * K * D
 
@@ -47,32 +48,33 @@ def tile_sde_kernel(tc, table, latent, offs, out):
 
         partial = [[held.tile([P, W], F32, name=f"partial{b}_{i}") for i in range(2)] for b in range(DB)]
         summed = [partial[b][(T - 1) % 2] for b in range(DB)]
-        lang = [held.tile([P, W], F32, name=f"lang{b}") for b in range(DB)]
-        lang_bf = [held.tile([P, W], BF16, name=f"lang_bf{b}") for b in range(DB)]
-        result = [held.tile([P, W], F32, name=f"result{b}") for b in range(DB)]
+        lang = held.tile([P, DB, W], F32, name="lang")
+        lang_bf = held.tile([P, DB, W], BF16, name="lang_bf")
+        divided = held.tile([P, W // P, D], F32, name="divided")
+        result = held.tile([P, DB, W], F32, name="result")
 
-        for first_word in range(0, W, PIECE):
-            piece = slice(first_word, first_word + PIECE)
+        for b in range(DB):
+            nc.vector.tensor_copy(partial[b][0][:], tables[b][:].indirect(offsets[:, 0 : W // 16]))
+
+        first_word = 0
+        for width in PIECES:
+            piece = slice(first_word, first_word + width)
 
             for b in range(DB):
-                for t in range(T):
+                for t in range(1, T):
                     first_col = (t * W + first_word) // 16
-                    picked = tables[b][:].indirect(offsets[:, first_col : first_col + PIECE // 16])
-                    if t == 0:
-                        nc.vector.tensor_copy(partial[b][0][:, piece], picked)
-                    else:
-                        nc.vector.tensor_tensor(
-                            partial[b][t % 2][:, piece], picked, partial[b][(t - 1) % 2][:, piece], ADD
-                        )
-                nc.scalar.activation(lang_bf[b][:, piece], summed[b][:, piece], ACT.Tanh, scale=1.0 / T)
-                nc.scalar.activation(lang[b][:, piece], summed[b][:, piece], ACT.Tanh, scale=1.0 / T)
+                    picked = tables[b][:].indirect(offsets[:, first_col : first_col + width // 16])
+                    nc.vector.tensor_tensor(
+                        partial[b][t % 2][:, piece], picked, partial[b][(t - 1) % 2][:, piece], ADD
+                    )
+                nc.scalar.activation(lang_bf[:, b, piece], summed[b][:, piece], ACT.Tanh, scale=1.0 / T)
 
-            for w in range(first_word, first_word + PIECE, P):
-                words = slice(w, w + P)
+            for i in range(first_word // P, (first_word + width) // P):
+                words = slice(i * P, (i + 1) * P)
                 scores = psum.tile([P, K], F32, name="scores")
                 for b in range(DB):
                     nc.tensor.matmul(
-                        scores[:], lang_bf[b][:, words], codesT[b][:], start=(b == 0), stop=(b == DB - 1)
+                        scores[:], lang_bf[:, b, words], codesT[b][:], start=(b == 0), stop=(b == DB - 1)
                     )
                 negmax = stats.tile([P, 1], F32, name="negmax")
                 nc.vector.reduce_max(negmax[:], scores[:], axis=X, negate=True)
@@ -94,14 +96,17 @@ def tile_sde_kernel(tc, table, latent, offs, out):
                     nc.tensor.matmul(
                         mix[:], weightsT[:, c * P : (c + 1) * P], codes[:, c, :], start=(c == 0), stop=(c == KB - 1)
                     )
-                divided = work.tile([P, D], F32, name="divided")
-                nc.scalar.activation(divided[:], mix[:], ACT.Copy, scale=inverse[:])
-
-                back = psum.tile([P, D], F32, name="back")
-                for b in range(DB):
-                    nc.tensor.transpose(back[:, b * P : (b + 1) * P], divided[:, b * P : (b + 1) * P], ident_f32[:])
-                for b in range(DB):
-                    nc.vector.tensor_tensor(result[b][:, words], back[:, b * P : (b + 1) * P], lang[b][:, words], ADD)
+                nc.scalar.activation(divided[:, i, :], mix[:], ACT.Copy, scale=inverse[:])
 
             for b in range(DB):
-                nc.sync.dma_start(out[b * P : (b + 1) * P, piece], result[b][:, piece])
+                nc.scalar.activation(lang[:, b, piece], summed[b][:, piece], ACT.Tanh, scale=1.0 / T)
+            first_word += width
+
+        out_blocks = out.rearrange("(b p) n -> p b n", p=P)
+        for i in range(W // P):
+            words = slice(i * P, (i + 1) * P)
+            back = psum.tile([P, DB, P], F32, name="back")
+            for b in range(DB):
+                nc.tensor.transpose(back[:, b, :], divided[:, i, b * P : (b + 1) * P], ident_f32[:])
+            nc.vector.tensor_tensor(result[:, :, words], back[:], lang[:, :, words], ADD)
+            nc.sync.dma_start(out_blocks[:, :, words], result[:, :, words])

@@ -1,10 +1,11 @@
+import math
+
 import concourse.mybir as mybir
 from concourse.masks import make_identity
 
-F32, BF16, U16 = mybir.dt.float32, mybir.dt.bfloat16, mybir.dt.uint16
-ADD = mybir.AluOpType.add
+F32, BF16, U16, U32 = mybir.dt.float32, mybir.dt.bfloat16, mybir.dt.uint16, mybir.dt.uint32
+ADD, POW = mybir.AluOpType.add, mybir.AluOpType.pow
 ACT = mybir.ActivationFunctionType
-X = mybir.AxisListType.X
 
 P = 128
 D, S, T, W, K = 256, 4096, 8, 1024, 512
@@ -12,6 +13,8 @@ DB = D // P
 KB = K // P
 PIECES = (256, 256, 256, 128, 128)
 assert sum(PIECES) == W
+STARTS = [sum(PIECES[:i]) for i in range(len(PIECES))]
+SOFT = 8.0
 
 FLOPS = 4 * W * K * D
 
@@ -20,6 +23,8 @@ def tile_sde_kernel(tc, table, latent, offs, out):
     nc = tc.nc
     with (
         tc.tile_pool(name="held", bufs=1) as held,
+        tc.tile_pool(name="sums", bufs=4) as sums,
+        tc.tile_pool(name="rounded", bufs=1) as rounded,
         tc.tile_pool(name="work", bufs=2) as work,
         tc.tile_pool(name="stats", bufs=4) as stats,
         tc.psum_pool(name="psum", bufs=2) as psum,
@@ -37,6 +42,9 @@ def tile_sde_kernel(tc, table, latent, offs, out):
         ident_f32 = held.tile([P, P], F32, name="ident_f32")
         make_identity(nc, ident_f32[:])
 
+        minus_one = held.tile([P, 1], F32, name="minus_one")
+        nc.gpsimd.memset(minus_one[:], -1.0)
+
         codesT = [held.tile([P, K], BF16, name=f"codesT{b}") for b in range(DB)]
         for b in range(DB):
             flipped = psum.tile([P, K], BF16, name="flipped")
@@ -46,61 +54,76 @@ def tile_sde_kernel(tc, table, latent, offs, out):
                 )
             nc.scalar.copy(codesT[b][:], flipped[:])
 
-        partial = [[held.tile([P, W], F32, name=f"partial{b}_{i}") for i in range(2)] for b in range(DB)]
-        summed = [partial[b][(T - 1) % 2] for b in range(DB)]
+        first = held.tile([P, DB, W], F32, name="first")
+        summed = held.tile([P, DB, W], F32, name="summed")
         lang = held.tile([P, DB, W], F32, name="lang")
-        lang_bf = held.tile([P, DB, W], BF16, name="lang_bf")
         divided = held.tile([P, W // P, D], F32, name="divided")
         result = held.tile([P, DB, W], F32, name="result")
 
         for b in range(DB):
-            nc.vector.tensor_copy(partial[b][0][:], tables[b][:].indirect(offsets[:, 0 : W // 16]))
+            nc.vector.tensor_copy(first[:, b, :], tables[b][:].indirect(offsets[:, 0 : W // 16]))
 
-        first_word = 0
-        for width in PIECES:
+        def look_up(j):
+            first_word, width = STARTS[j], PIECES[j]
             piece = slice(first_word, first_word + width)
-
-            for b in range(DB):
-                for t in range(1, T):
-                    first_col = (t * W + first_word) // 16
-                    picked = tables[b][:].indirect(offsets[:, first_col : first_col + width // 16])
-                    nc.vector.tensor_tensor(
-                        partial[b][t % 2][:, piece], picked, partial[b][(t - 1) % 2][:, piece], ADD
-                    )
-                nc.scalar.activation(lang_bf[:, b, piece], summed[b][:, piece], ACT.Tanh, scale=1.0 / T)
-
-            for i in range(first_word // P, (first_word + width) // P):
-                words = slice(i * P, (i + 1) * P)
-                scores = psum.tile([P, K], F32, name="scores")
+            running = first[:, :, piece]
+            for t in range(1, T):
+                first_col = (t * W + first_word) // 16
+                if t < T - 1:
+                    partial = sums.tile([P, DB, width], F32, name=f"partial{j % 2}")[:]
+                else:
+                    partial = summed[:, :, piece]
                 for b in range(DB):
-                    nc.tensor.matmul(
-                        scores[:], lang_bf[:, b, words], codesT[b][:], start=(b == 0), stop=(b == DB - 1)
-                    )
-                negmax = stats.tile([P, 1], F32, name="negmax")
-                nc.vector.reduce_max(negmax[:], scores[:], axis=X, negate=True)
-                weights = work.tile([P, K], BF16, name="weights")
-                total = stats.tile([P, 1], F32, name="total")
-                nc.scalar.activation(weights[:], scores[:], ACT.Exp, bias=negmax[:], accum_out=total[:])
-                inverse = stats.tile([P, 1], F32, name="inverse")
-                nc.vector.reciprocal(inverse[:], total[:])
+                    picked = tables[b][:].indirect(offsets[:, first_col : first_col + width // 16])
+                    nc.vector.tensor_tensor(partial[:, b, :], picked, running[:, b, :], ADD)
+                running = partial
+            lang_bf = rounded.tile([P, DB, width], BF16, name="lang_bf")
+            nc.scalar.activation(lang_bf[:], summed[:, :, piece], ACT.Tanh, scale=1.0 / T)
+            return lang_bf
 
-                flipped = psum.tile([P, K], BF16, name="flipped")
-                for c in range(KB):
-                    nc.tensor.transpose(
-                        flipped[:, c * P : (c + 1) * P], weights[:, c * P : (c + 1) * P], ident_bf[:]
-                    )
-                weightsT = work.tile([P, K], BF16, name="weightsT")
-                nc.scalar.copy(weightsT[:], flipped[:])
-                mix = psum.tile([P, D], F32, name="mix")
-                for c in range(KB):
-                    nc.tensor.matmul(
-                        mix[:], weightsT[:, c * P : (c + 1) * P], codes[:, c, :], start=(c == 0), stop=(c == KB - 1)
-                    )
-                nc.scalar.activation(divided[:, i, :], mix[:], ACT.Copy, scale=inverse[:])
-
+        def softmax_and_mix(i, lang_block):
+            scores = psum.tile([P, K], F32, name="scores")
             for b in range(DB):
-                nc.scalar.activation(lang[:, b, piece], summed[b][:, piece], ACT.Tanh, scale=1.0 / T)
-            first_word += width
+                nc.tensor.matmul(
+                    scores[:], lang_block[:, b, :], codesT[b][:], start=(b == 0), stop=(b == DB - 1)
+                )
+            tempered = work.tile([P, K], BF16, name="tempered")
+            tempered_sum = stats.tile([P, 1], F32, name="tempered_sum")
+            nc.scalar.activation(tempered[:], scores[:], ACT.Exp, scale=1.0 / SOFT, accum_out=tempered_sum[:])
+            negshift = stats.tile([P, 1], F32, name="negshift")
+            nc.scalar.activation(
+                negshift[:],
+                tempered_sum[:].bitcast(U32),
+                ACT.Copy,
+                scale=-SOFT * math.log(2.0) / 2.0**23,
+                bias=SOFT * math.log(2.0) * 127.0,
+            )
+            weights = work.tile([P, K], BF16, name="weights")
+            total = stats.tile([P, 1], F32, name="total")
+            nc.scalar.activation(weights[:], scores[:], ACT.Exp, bias=negshift[:], accum_out=total[:])
+            inverse = stats.tile([P, 1], F32, name="inverse")
+            nc.gpsimd.tensor_tensor(inverse[:], total[:], minus_one[:], POW)
+
+            flipped = psum.tile([P, K], BF16, name="flipped")
+            for c in range(KB):
+                nc.tensor.transpose(
+                    flipped[:, c * P : (c + 1) * P], weights[:, c * P : (c + 1) * P], ident_bf[:]
+                )
+            weightsT = work.tile([P, K], BF16, name="weightsT")
+            nc.scalar.copy(weightsT[:], flipped[:])
+            mix = psum.tile([P, D], F32, name="mix")
+            for c in range(KB):
+                nc.tensor.matmul(
+                    mix[:], weightsT[:, c * P : (c + 1) * P], codes[:, c, :], start=(c == 0), stop=(c == KB - 1)
+                )
+            nc.scalar.activation(divided[:, i, :], mix[:], ACT.Copy, scale=inverse[:])
+
+        for j in range(len(PIECES)):
+            lang_bf = look_up(j)
+            for i in range(PIECES[j] // P):
+                softmax_and_mix(STARTS[j] // P + i, lang_bf[:, :, i * P : (i + 1) * P])
+            piece = slice(STARTS[j], STARTS[j] + PIECES[j])
+            nc.scalar.activation(lang[:, :, piece], summed[:, :, piece], ACT.Tanh, scale=1.0 / T)
 
         out_blocks = out.rearrange("(b p) n -> p b n", p=P)
         for i in range(W // P):

@@ -4,7 +4,7 @@ import concourse.mybir as mybir
 from concourse.masks import make_identity
 
 F32, BF16, U16, U32 = mybir.dt.float32, mybir.dt.bfloat16, mybir.dt.uint16, mybir.dt.uint32
-ADD, POW = mybir.AluOpType.add, mybir.AluOpType.pow
+ADD = mybir.AluOpType.add
 ACT = mybir.ActivationFunctionType
 
 P = 128
@@ -41,9 +41,6 @@ def tile_sde_kernel(tc, table, latent, offs, out):
         make_identity(nc, ident_bf[:])
         ident_f32 = held.tile([P, P], F32, name="ident_f32")
         make_identity(nc, ident_f32[:])
-
-        minus_one = held.tile([P, 1], F32, name="minus_one")
-        nc.gpsimd.memset(minus_one[:], -1.0)
 
         codesT = [held.tile([P, K], BF16, name=f"codesT{b}") for b in range(DB)]
         for b in range(DB):
@@ -102,7 +99,7 @@ def tile_sde_kernel(tc, table, latent, offs, out):
             total = stats.tile([P, 1], F32, name="total")
             nc.scalar.activation(weights[:], scores[:], ACT.Exp, bias=negshift[:], accum_out=total[:])
             inverse = stats.tile([P, 1], F32, name="inverse")
-            nc.gpsimd.tensor_tensor(inverse[:], total[:], minus_one[:], POW)
+            nc.vector.reciprocal(inverse[:], total[:])
 
             flipped = psum.tile([P, K], BF16, name="flipped")
             for c in range(KB):

@@ -52,9 +52,10 @@ def tile_sde_kernel(tc, table, latent, offs, out):
             nc.scalar.copy(codesT[b][:], flipped[:])
 
         first = held.tile([P, DB, W], F32, name="first")
-        summed = held.tile([P, DB, W], F32, name="summed")
         lang = held.tile([P, DB, W], F32, name="lang")
-        divided = held.tile([P, W // P, D], F32, name="divided")
+        mixed = held.tile([P, W // P, D], F32, name="mixed")
+        totals = held.tile([P, W // P], F32, name="totals")
+        inverses = held.tile([P, W // P], F32, name="inverses")
         result = held.tile([P, DB, W], F32, name="result")
 
         for b in range(DB):
@@ -69,13 +70,14 @@ def tile_sde_kernel(tc, table, latent, offs, out):
                 if t < T - 1:
                     partial = sums.tile([P, DB, width], F32, name=f"partial{j % 2}")[:]
                 else:
-                    partial = summed[:, :, piece]
+                    partial = lang[:, :, piece]
                 for b in range(DB):
                     picked = tables[b][:].indirect(offsets[:, first_col : first_col + width // 16])
                     nc.vector.tensor_tensor(partial[:, b, :], picked, running[:, b, :], ADD)
                 running = partial
             lang_bf = rounded.tile([P, DB, width], BF16, name="lang_bf")
-            nc.scalar.activation(lang_bf[:], summed[:, :, piece], ACT.Tanh, scale=1.0 / T)
+            nc.scalar.activation(lang_bf[:], lang[:, :, piece], ACT.Tanh, scale=1.0 / T)
+            nc.scalar.activation(lang[:, :, piece], lang[:, :, piece], ACT.Tanh, scale=1.0 / T)
             return lang_bf
 
         def softmax_and_mix(i, lang_block):
@@ -96,10 +98,9 @@ def tile_sde_kernel(tc, table, latent, offs, out):
                 bias=SOFT * math.log(2.0) * 127.0,
             )
             weights = work.tile([P, K], BF16, name="weights")
-            total = stats.tile([P, 1], F32, name="total")
-            nc.scalar.activation(weights[:], scores[:], ACT.Exp, bias=negshift[:], accum_out=total[:])
-            inverse = stats.tile([P, 1], F32, name="inverse")
-            nc.vector.reciprocal(inverse[:], total[:])
+            nc.scalar.activation(
+                weights[:], scores[:], ACT.Exp, bias=negshift[:], accum_out=totals[:, i : i + 1]
+            )
 
             flipped = psum.tile([P, K], BF16, name="flipped")
             for c in range(KB):
@@ -113,20 +114,25 @@ def tile_sde_kernel(tc, table, latent, offs, out):
                 nc.tensor.matmul(
                     mix[:], weightsT[:, c * P : (c + 1) * P], codes[:, c, :], start=(c == 0), stop=(c == KB - 1)
                 )
-            nc.scalar.activation(divided[:, i, :], mix[:], ACT.Copy, scale=inverse[:])
+            nc.scalar.copy(mixed[:, i, :], mix[:])
 
         for j in range(len(PIECES)):
             lang_bf = look_up(j)
             for i in range(PIECES[j] // P):
                 softmax_and_mix(STARTS[j] // P + i, lang_bf[:, :, i * P : (i + 1) * P])
-            piece = slice(STARTS[j], STARTS[j] + PIECES[j])
-            nc.scalar.activation(lang[:, :, piece], summed[:, :, piece], ACT.Tanh, scale=1.0 / T)
 
+        last_piece = STARTS[-1] // P
         out_blocks = out.rearrange("(b p) n -> p b n", p=P)
         for i in range(W // P):
+            if i == 0:
+                nc.vector.reciprocal(inverses[:, :last_piece], totals[:, :last_piece])
+            if i == last_piece:
+                nc.vector.reciprocal(inverses[:, last_piece:], totals[:, last_piece:])
             words = slice(i * P, (i + 1) * P)
+            divided = work.tile([P, D], F32, name="divided")
+            nc.vector.tensor_scalar_mul(divided[:], mixed[:, i, :], inverses[:, i : i + 1])
             back = psum.tile([P, DB, P], F32, name="back")
             for b in range(DB):
-                nc.tensor.transpose(back[:, b, :], divided[:, i, b * P : (b + 1) * P], ident_f32[:])
+                nc.tensor.transpose(back[:, b, :], divided[:, b * P : (b + 1) * P], ident_f32[:])
             nc.vector.tensor_tensor(result[:, :, words], back[:], lang[:, :, words], ADD)
             nc.sync.dma_start(out_blocks[:, :, words], result[:, :, words])

@@ -6,6 +6,7 @@ from concourse.masks import make_identity
 F32, BF16, U16, U32 = mybir.dt.float32, mybir.dt.bfloat16, mybir.dt.uint16, mybir.dt.uint32
 ADD = mybir.AluOpType.add
 ACT = mybir.ActivationFunctionType
+X = mybir.AxisListType.X
 
 P = 128
 D, S, T, W, K = 256, 4096, 8, 1024, 512
@@ -76,27 +77,33 @@ def tile_sde_kernel(tc, table, latent, offs, out):
                     nc.vector.tensor_tensor(partial[:, b, :], picked, running[:, b, :], ADD)
                 running = partial
             lang_bf = rounded.tile([P, DB, width], BF16, name="lang_bf")
-            nc.scalar.activation(lang_bf[:], lang[:, :, piece], ACT.Tanh, scale=1.0 / T)
+            for b in range(DB):
+                nc.scalar.activation(lang_bf[:, b, :], lang[:, b, piece], ACT.Tanh, scale=1.0 / T)
             nc.scalar.activation(lang[:, :, piece], lang[:, :, piece], ACT.Tanh, scale=1.0 / T)
             return lang_bf
 
-        def softmax_and_mix(i, lang_block):
+        def softmax_and_mix(i, lang_block, look_ups_done):
             scores = psum.tile([P, K], F32, name="scores")
             for b in range(DB):
                 nc.tensor.matmul(
                     scores[:], lang_block[:, b, :], codesT[b][:], start=(b == 0), stop=(b == DB - 1)
                 )
-            tempered = work.tile([P, K], BF16, name="tempered")
-            tempered_sum = stats.tile([P, 1], F32, name="tempered_sum")
-            nc.scalar.activation(tempered[:], scores[:], ACT.Exp, scale=1.0 / SOFT, accum_out=tempered_sum[:])
             negshift = stats.tile([P, 1], F32, name="negshift")
-            nc.scalar.activation(
-                negshift[:],
-                tempered_sum[:].bitcast(U32),
-                ACT.Copy,
-                scale=-SOFT * math.log(2.0) / 2.0**23,
-                bias=SOFT * math.log(2.0) * 127.0,
-            )
+            if look_ups_done:
+                nc.vector.reduce_max(negshift[:], scores[:], axis=X, negate=True)
+            else:
+                tempered = work.tile([P, K], BF16, name="tempered")
+                tempered_sum = stats.tile([P, 1], F32, name="tempered_sum")
+                nc.scalar.activation(
+                    tempered[:], scores[:], ACT.Exp, scale=1.0 / SOFT, accum_out=tempered_sum[:]
+                )
+                nc.scalar.activation(
+                    negshift[:],
+                    tempered_sum[:].bitcast(U32),
+                    ACT.Copy,
+                    scale=-SOFT * math.log(2.0) / 2.0**23,
+                    bias=SOFT * math.log(2.0) * 127.0,
+                )
             weights = work.tile([P, K], BF16, name="weights")
             nc.scalar.activation(
                 weights[:], scores[:], ACT.Exp, bias=negshift[:], accum_out=totals[:, i : i + 1]
@@ -114,23 +121,27 @@ def tile_sde_kernel(tc, table, latent, offs, out):
                 nc.tensor.matmul(
                     mix[:], weightsT[:, c * P : (c + 1) * P], codes[:, c, :], start=(c == 0), stop=(c == KB - 1)
                 )
+            if look_ups_done:
+                return mix[:]
             nc.scalar.copy(mixed[:, i, :], mix[:])
+            return mixed[:, i, :]
 
+        undivided = []
         for j in range(len(PIECES)):
             lang_bf = look_up(j)
             for i in range(PIECES[j] // P):
-                softmax_and_mix(STARTS[j] // P + i, lang_bf[:, :, i * P : (i + 1) * P])
+                undivided.append(
+                    softmax_and_mix(STARTS[j] // P + i, lang_bf[:, :, i * P : (i + 1) * P], j == len(PIECES) - 1)
+                )
 
-        last_piece = STARTS[-1] // P
+        groups = {0: STARTS[-2] // P, STARTS[-2] // P: STARTS[-1] // P, STARTS[-1] // P: W // P}
         out_blocks = out.rearrange("(b p) n -> p b n", p=P)
         for i in range(W // P):
-            if i == 0:
-                nc.vector.reciprocal(inverses[:, :last_piece], totals[:, :last_piece])
-            if i == last_piece:
-                nc.vector.reciprocal(inverses[:, last_piece:], totals[:, last_piece:])
+            if i in groups:
+                nc.vector.reciprocal(inverses[:, i : groups[i]], totals[:, i : groups[i]])
             words = slice(i * P, (i + 1) * P)
             divided = work.tile([P, D], F32, name="divided")
-            nc.vector.tensor_scalar_mul(divided[:], mixed[:, i, :], inverses[:, i : i + 1])
+            nc.vector.tensor_scalar_mul(divided[:], undivided[i], inverses[:, i : i + 1])
             back = psum.tile([P, DB, P], F32, name="back")
             for b in range(DB):
                 nc.tensor.transpose(back[:, b, :], divided[:, b * P : (b + 1) * P], ident_f32[:])

@@ -105,9 +105,17 @@ def tile_sde_kernel(tc, table, latent, offs, out):
                     bias=SOFT * math.log(2.0) * 127.0,
                 )
             weights = work.tile([P, K], BF16, name="weights")
-            nc.scalar.activation(
-                weights[:], scores[:], ACT.Exp, bias=negshift[:], accum_out=totals[:, i : i + 1]
-            )
+            if look_ups_done:
+                exps = work.tile([P, K], F32, name="exps")
+                nc.scalar.activation(
+                    exps[:], scores[:], ACT.Exp, bias=negshift[:], accum_out=totals[:, i : i + 1]
+                )
+                nc.vector.reciprocal(inverses[:, i : i + 1], totals[:, i : i + 1])
+                nc.vector.tensor_scalar_mul(weights[:], exps[:], inverses[:, i : i + 1])
+            else:
+                nc.scalar.activation(
+                    weights[:], scores[:], ACT.Exp, bias=negshift[:], accum_out=totals[:, i : i + 1]
+                )
 
             flipped = psum.tile([P, K], BF16, name="flipped")
             for c in range(KB):
@@ -117,12 +125,19 @@ def tile_sde_kernel(tc, table, latent, offs, out):
             weightsT = work.tile([P, K], BF16, name="weightsT")
             nc.scalar.copy(weightsT[:], flipped[:])
             mix = psum.tile([P, D], F32, name="mix")
+            if look_ups_done:
+                for b in range(DB):
+                    features = slice(b * P, (b + 1) * P)
+                    for c in range(KB):
+                        nc.tensor.matmul(
+                            mix[:, features], codes[:, c, features], weightsT[:, c * P : (c + 1) * P],
+                            start=(c == 0), stop=(c == KB - 1),
+                        )
+                return mix[:].rearrange("p (b n) -> p b n", b=DB)
             for c in range(KB):
                 nc.tensor.matmul(
                     mix[:], weightsT[:, c * P : (c + 1) * P], codes[:, c, :], start=(c == 0), stop=(c == KB - 1)
                 )
-            if look_ups_done:
-                return mix[:]
             nc.scalar.copy(mixed[:, i, :], mix[:])
             return mixed[:, i, :]
 
@@ -134,12 +149,16 @@ def tile_sde_kernel(tc, table, latent, offs, out):
                     softmax_and_mix(STARTS[j] // P + i, lang_bf[:, :, i * P : (i + 1) * P], j == len(PIECES) - 1)
                 )
 
-        groups = {0: STARTS[-2] // P, STARTS[-2] // P: STARTS[-1] // P, STARTS[-1] // P: W // P}
+        groups = {0: STARTS[-2] // P, STARTS[-2] // P: STARTS[-1] // P}
         out_blocks = out.rearrange("(b p) n -> p b n", p=P)
         for i in range(W // P):
             if i in groups:
                 nc.vector.reciprocal(inverses[:, i : groups[i]], totals[:, i : groups[i]])
             words = slice(i * P, (i + 1) * P)
+            if i >= STARTS[-1] // P:
+                nc.vector.tensor_tensor(result[:, :, words], undivided[i], lang[:, :, words], ADD)
+                nc.sync.dma_start(out_blocks[:, :, words], result[:, :, words])
+                continue
             divided = work.tile([P, D], F32, name="divided")
             nc.vector.tensor_scalar_mul(divided[:], undivided[i], inverses[:, i : i + 1])
             back = psum.tile([P, DB, P], F32, name="back")

@@ -12,9 +12,12 @@ P = 128
 D, S, T, W, K = 256, 4096, 8, 1024, 512
 DB = D // P
 KB = K // P
-PIECES = (256, 256, 256, 128, 128)
+GROUPS = ((256, 256), (256,), (128, 128))
+PIECES = [width for group in GROUPS for width in group]
 assert sum(PIECES) == W
 STARTS = [sum(PIECES[:i]) for i in range(len(PIECES))]
+HALF = W // 2
+EARLY = T // 2
 SOFT = 8.0
 
 FLOPS = 4 * W * K * D
@@ -24,7 +27,8 @@ def tile_sde_kernel(tc, table, latent, offs, out):
     nc = tc.nc
     with (
         tc.tile_pool(name="held", bufs=1) as held,
-        tc.tile_pool(name="sums", bufs=4) as sums,
+        tc.tile_pool(name="early", bufs=3) as early_sums,
+        tc.tile_pool(name="late", bufs=4) as late_sums,
         tc.tile_pool(name="rounded", bufs=1) as rounded,
         tc.tile_pool(name="work", bufs=2) as work,
         tc.tile_pool(name="stats", bufs=4) as stats,
@@ -52,30 +56,38 @@ def tile_sde_kernel(tc, table, latent, offs, out):
                 )
             nc.scalar.copy(codesT[b][:], flipped[:])
 
-        first = held.tile([P, DB, W], F32, name="first")
         lang = held.tile([P, DB, W], F32, name="lang")
         mixed = held.tile([P, W // P, D], F32, name="mixed")
         totals = held.tile([P, W // P], F32, name="totals")
         inverses = held.tile([P, W // P], F32, name="inverses")
         result = held.tile([P, DB, W], F32, name="result")
 
-        for b in range(DB):
-            nc.vector.tensor_copy(first[:, b, :], tables[b][:].indirect(offsets[:, 0 : W // 16]))
+        def first_terms(words, ring):
+            width = words.stop - words.start
+            first = ring.tile([P, DB, width], F32, name="partial")
+            for b in range(DB):
+                picked = tables[b][:].indirect(offsets[:, words.start // 16 : words.stop // 16])
+                nc.vector.tensor_copy(first[:, b, :], picked)
+            return first
 
-        def look_up(j):
-            first_word, width = STARTS[j], PIECES[j]
-            piece = slice(first_word, first_word + width)
-            running = first[:, :, piece]
-            for t in range(1, T):
-                first_col = (t * W + first_word) // 16
-                if t < T - 1:
-                    partial = sums.tile([P, DB, width], F32, name=f"partial{j % 2}")[:]
+        def add_terms(terms, words, running, last, ring):
+            width = words.stop - words.start
+            for t in terms:
+                first_col = (t * W + words.start) // 16
+                if last is None or t < terms[-1]:
+                    partial = ring.tile([P, DB, width], F32, name="partial")[:]
                 else:
-                    partial = lang[:, :, piece]
+                    partial = last
                 for b in range(DB):
                     picked = tables[b][:].indirect(offsets[:, first_col : first_col + width // 16])
                     nc.vector.tensor_tensor(partial[:, b, :], picked, running[:, b, :], ADD)
                 running = partial
+            return running
+
+        def look_up(j, early):
+            width = PIECES[j]
+            piece = slice(STARTS[j], STARTS[j] + width)
+            add_terms(range(EARLY, T), piece, early, lang[:, :, piece], late_sums)
             lang_bf = rounded.tile([P, DB, width], BF16, name="lang_bf")
             for b in range(DB):
                 nc.scalar.activation(lang_bf[:, b, :], lang[:, b, piece], ACT.Tanh, scale=1.0 / T)
@@ -142,12 +154,22 @@ def tile_sde_kernel(tc, table, latent, offs, out):
             return mixed[:, i, :]
 
         undivided = []
-        for j in range(len(PIECES)):
-            lang_bf = look_up(j)
-            for i in range(PIECES[j] // P):
-                undivided.append(
-                    softmax_and_mix(STARTS[j] // P + i, lang_bf[:, :, i * P : (i + 1) * P], j == len(PIECES) - 1)
-                )
+        j = 0
+        for group in GROUPS:
+            start = STARTS[j]
+            words = slice(start, start + sum(group))
+            if start % HALF == 0:
+                first = first_terms(slice(start, start + HALF), early_sums if start == 0 else held)
+            terms_before = first[:, :, start % HALF : start % HALF + sum(group)]
+            early = add_terms(range(1, EARLY), words, terms_before, None, early_sums)
+            for width in group:
+                piece_early = early[:, :, STARTS[j] - start : STARTS[j] - start + width]
+                lang_bf = look_up(j, piece_early)
+                for i in range(width // P):
+                    undivided.append(
+                        softmax_and_mix(STARTS[j] // P + i, lang_bf[:, :, i * P : (i + 1) * P], j == len(PIECES) - 1)
+                    )
+                j += 1
 
         groups = {0: STARTS[-2] // P, STARTS[-2] // P: STARTS[-1] // P}
         out_blocks = out.rearrange("(b p) n -> p b n", p=P)

@@ -29,7 +29,6 @@ def tile_sde_kernel(tc, table, latent, offs, out):
         tc.tile_pool(name="held", bufs=1) as held,
         tc.tile_pool(name="early", bufs=3) as early_sums,
         tc.tile_pool(name="late", bufs=4) as late_sums,
-        tc.tile_pool(name="rounded", bufs=1) as rounded,
         tc.tile_pool(name="work", bufs=2) as work,
         tc.tile_pool(name="stats", bufs=4) as stats,
         tc.psum_pool(name="psum", bufs=2) as psum,
@@ -84,24 +83,26 @@ def tile_sde_kernel(tc, table, latent, offs, out):
                 running = partial
             return running
 
+        operands = held.tile([P, max(PIECES) // P, K], BF16, name="operands")
+
         def look_up(j, early):
             width = PIECES[j]
             piece = slice(STARTS[j], STARTS[j] + width)
             add_terms(range(EARLY, T), piece, early, lang[:, :, piece], late_sums)
-            lang_bf = rounded.tile([P, DB, width], BF16, name="lang_bf")
+            lang_bf = operands[:, max(PIECES) // P - 1, : DB * width].rearrange("p (b n) -> p b n", b=DB)
             for b in range(DB):
                 nc.scalar.activation(lang_bf[:, b, :], lang[:, b, piece], ACT.Tanh, scale=1.0 / T)
             nc.scalar.activation(lang[:, :, piece], lang[:, :, piece], ACT.Tanh, scale=1.0 / T)
             return lang_bf
 
-        def softmax_and_mix(i, lang_block, look_ups_done):
+        def softmax_and_mix(i, lang_block, weights, maximum, divide_first):
             scores = psum.tile([P, K], F32, name="scores")
             for b in range(DB):
                 nc.tensor.matmul(
                     scores[:], lang_block[:, b, :], codesT[b][:], start=(b == 0), stop=(b == DB - 1)
                 )
             negshift = stats.tile([P, 1], F32, name="negshift")
-            if look_ups_done:
+            if maximum:
                 nc.vector.reduce_max(negshift[:], scores[:], axis=X, negate=True)
             else:
                 tempered = work.tile([P, K], BF16, name="tempered")
@@ -116,17 +117,16 @@ def tile_sde_kernel(tc, table, latent, offs, out):
                     scale=-SOFT * math.log(2.0) / 2.0**23,
                     bias=SOFT * math.log(2.0) * 127.0,
                 )
-            weights = work.tile([P, K], BF16, name="weights")
-            if look_ups_done:
+            if divide_first:
                 exps = work.tile([P, K], F32, name="exps")
                 nc.scalar.activation(
                     exps[:], scores[:], ACT.Exp, bias=negshift[:], accum_out=totals[:, i : i + 1]
                 )
                 nc.vector.reciprocal(inverses[:, i : i + 1], totals[:, i : i + 1])
-                nc.vector.tensor_scalar_mul(weights[:], exps[:], inverses[:, i : i + 1])
+                nc.vector.tensor_scalar_mul(weights, exps[:], inverses[:, i : i + 1])
             else:
                 nc.scalar.activation(
-                    weights[:], scores[:], ACT.Exp, bias=negshift[:], accum_out=totals[:, i : i + 1]
+                    weights, scores[:], ACT.Exp, bias=negshift[:], accum_out=totals[:, i : i + 1]
                 )
 
             flipped = psum.tile([P, K], BF16, name="flipped")
@@ -137,7 +137,7 @@ def tile_sde_kernel(tc, table, latent, offs, out):
             weightsT = work.tile([P, K], BF16, name="weightsT")
             nc.scalar.copy(weightsT[:], flipped[:])
             mix = psum.tile([P, D], F32, name="mix")
-            if look_ups_done:
+            if divide_first:
                 for b in range(DB):
                     features = slice(b * P, (b + 1) * P)
                     for c in range(KB):
@@ -153,7 +153,7 @@ def tile_sde_kernel(tc, table, latent, offs, out):
             nc.scalar.copy(mixed[:, i, :], mix[:])
             return mixed[:, i, :]
 
-        undivided = []
+        mixes = []
         j = 0
         for group in GROUPS:
             start = STARTS[j]
@@ -166,25 +166,30 @@ def tile_sde_kernel(tc, table, latent, offs, out):
                 piece_early = early[:, :, STARTS[j] - start : STARTS[j] - start + width]
                 lang_bf = look_up(j, piece_early)
                 for i in range(width // P):
-                    undivided.append(
-                        softmax_and_mix(STARTS[j] // P + i, lang_bf[:, :, i * P : (i + 1) * P], j == len(PIECES) - 1)
+                    if j < len(PIECES) - 2:
+                        weights = operands[:, i, :]
+                    else:
+                        weights = work.tile([P, K], BF16, name="weights")[:]
+                    lang_block = lang_bf[:, :, i * P : (i + 1) * P]
+                    mixes.append(
+                        softmax_and_mix(
+                            STARTS[j] // P + i, lang_block, weights, j == len(PIECES) - 1, j >= len(PIECES) - 2
+                        )
                     )
                 j += 1
 
-        groups = {0: STARTS[-2] // P, STARTS[-2] // P: STARTS[-1] // P}
+        late_blocks = STARTS[-2] // P
+        nc.vector.reciprocal(inverses[:, :late_blocks], totals[:, :late_blocks])
         out_blocks = out.rearrange("(b p) n -> p b n", p=P)
         for i in range(W // P):
-            if i in groups:
-                nc.vector.reciprocal(inverses[:, i : groups[i]], totals[:, i : groups[i]])
+            mix = mixes[i]
+            if i < late_blocks:
+                divided = work.tile([P, D], F32, name="divided")
+                nc.vector.tensor_scalar_mul(divided[:], mix, inverses[:, i : i + 1])
+                back = psum.tile([P, DB, P], F32, name="back")
+                for b in range(DB):
+                    nc.tensor.transpose(back[:, b, :], divided[:, b * P : (b + 1) * P], ident_f32[:])
+                mix = back[:]
             words = slice(i * P, (i + 1) * P)
-            if i >= STARTS[-1] // P:
-                nc.vector.tensor_tensor(result[:, :, words], undivided[i], lang[:, :, words], ADD)
-                nc.sync.dma_start(out_blocks[:, :, words], result[:, :, words])
-                continue
-            divided = work.tile([P, D], F32, name="divided")
-            nc.vector.tensor_scalar_mul(divided[:], undivided[i], inverses[:, i : i + 1])
-            back = psum.tile([P, DB, P], F32, name="back")
-            for b in range(DB):
-                nc.tensor.transpose(back[:, b, :], divided[:, b * P : (b + 1) * P], ident_f32[:])
-            nc.vector.tensor_tensor(result[:, :, words], back[:], lang[:, :, words], ADD)
+            nc.vector.tensor_tensor(result[:, :, words], mix, lang[:, :, words], ADD)
             nc.sync.dma_start(out_blocks[:, :, words], result[:, :, words])

@@ -105,10 +105,10 @@ def tile_sde_kernel(tc, table, latent, offs, out):
             if maximum:
                 nc.vector.reduce_max(negshift[:], scores[:], axis=X, negate=True)
             else:
-                tempered = work.tile([P, K], BF16, name="tempered")
+                tempered = operands[:, max(PIECES) // P - 1, :] if divide_first else work.tile([P, K], BF16, name="tempered")[:]
                 tempered_sum = stats.tile([P, 1], F32, name="tempered_sum")
                 nc.scalar.activation(
-                    tempered[:], scores[:], ACT.Exp, scale=1.0 / SOFT, accum_out=tempered_sum[:]
+                    tempered, scores[:], ACT.Exp, scale=1.0 / SOFT, accum_out=tempered_sum[:]
                 )
                 nc.scalar.activation(
                     negshift[:],
@@ -180,16 +180,22 @@ def tile_sde_kernel(tc, table, latent, offs, out):
 
         late_blocks = STARTS[-2] // P
         nc.vector.reciprocal(inverses[:, :late_blocks], totals[:, :late_blocks])
+        divided = held.tile([P, late_blocks, D], F32, name="divided")
+        for i in range(late_blocks):
+            nc.vector.tensor_scalar_mul(divided[:, i, :], mixes[i], inverses[:, i : i + 1])
+        late_ident = lang_bf.rearrange("p b n -> p (b n)").bitcast(F32)
+        nc.vector.tensor_copy(late_ident, ident_f32[:])
         out_blocks = out.rearrange("(b p) n -> p b n", p=P)
-        for i in range(W // P):
-            mix = mixes[i]
-            if i < late_blocks:
-                divided = work.tile([P, D], F32, name="divided")
-                nc.vector.tensor_scalar_mul(divided[:], mix, inverses[:, i : i + 1])
-                back = psum.tile([P, DB, P], F32, name="back")
-                for b in range(DB):
-                    nc.tensor.transpose(back[:, b, :], divided[:, b * P : (b + 1) * P], ident_f32[:])
+        for j in range(len(PIECES)):
+            words = slice(STARTS[j], STARTS[j] + PIECES[j])
+            if j < len(PIECES) - 2:
+                back = psum.tile([P, DB, PIECES[j]], F32, name="back")
+                for i in range(words.start // P, words.stop // P):
+                    columns = slice(i * P - words.start, (i + 1) * P - words.start)
+                    for b in range(DB):
+                        nc.tensor.transpose(back[:, b, columns], divided[:, i, b * P : (b + 1) * P], late_ident)
                 mix = back[:]
-            words = slice(i * P, (i + 1) * P)
+            else:
+                mix = mixes[words.start // P]
             nc.vector.tensor_tensor(result[:, :, words], mix, lang[:, :, words], ADD)
             nc.sync.dma_start(out_blocks[:, :, words], result[:, :, words])

@@ -95,17 +95,21 @@ def tile_sde_kernel(tc, table, latent, offs, out):
             nc.scalar.activation(lang[:, :, piece], lang[:, :, piece], ACT.Tanh, scale=1.0 / T)
             return lang_bf
 
-        def softmax_and_mix(i, lang_block, weights, maximum, divide_first):
+        def late_ident(lang_block):
+            return lang_block.rearrange("p b n -> p (b n)").bitcast(F32)
+
+        def softmax_and_mix(i, lang_block, weights, left):
             scores = psum.tile([P, K], F32, name="scores")
             for b in range(DB):
                 nc.tensor.matmul(
                     scores[:], lang_block[:, b, :], codesT[b][:], start=(b == 0), stop=(b == DB - 1)
                 )
             negshift = stats.tile([P, 1], F32, name="negshift")
-            if maximum:
+            if left == 0:
+                nc.vector.tensor_copy(late_ident(lang_block), ident_f32[:])
                 nc.vector.reduce_max(negshift[:], scores[:], axis=X, negate=True)
             else:
-                tempered = operands[:, max(PIECES) // P - 1, :] if divide_first else work.tile([P, K], BF16, name="tempered")[:]
+                tempered = operands[:, max(PIECES) // P - 1, :] if left == 1 else work.tile([P, K], BF16, name="tempered")[:]
                 tempered_sum = stats.tile([P, 1], F32, name="tempered_sum")
                 nc.scalar.activation(
                     tempered, scores[:], ACT.Exp, scale=1.0 / SOFT, accum_out=tempered_sum[:]
@@ -117,7 +121,7 @@ def tile_sde_kernel(tc, table, latent, offs, out):
                     scale=-SOFT * math.log(2.0) / 2.0**23,
                     bias=SOFT * math.log(2.0) * 127.0,
                 )
-            if divide_first:
+            if left == 0:
                 exps = work.tile([P, K], F32, name="exps")
                 nc.scalar.activation(
                     exps[:], scores[:], ACT.Exp, bias=negshift[:], accum_out=totals[:, i : i + 1]
@@ -137,7 +141,7 @@ def tile_sde_kernel(tc, table, latent, offs, out):
             weightsT = work.tile([P, K], BF16, name="weightsT")
             nc.scalar.copy(weightsT[:], flipped[:])
             mix = psum.tile([P, D], F32, name="mix")
-            if divide_first:
+            if left == 0:
                 for b in range(DB):
                     features = slice(b * P, (b + 1) * P)
                     for c in range(KB):
@@ -150,6 +154,8 @@ def tile_sde_kernel(tc, table, latent, offs, out):
                 nc.tensor.matmul(
                     mix[:], weightsT[:, c * P : (c + 1) * P], codes[:, c, :], start=(c == 0), stop=(c == KB - 1)
                 )
+            if left == 1:
+                return mix[:]
             nc.scalar.copy(mixed[:, i, :], mix[:])
             return mixed[:, i, :]
 
@@ -171,31 +177,24 @@ def tile_sde_kernel(tc, table, latent, offs, out):
                     else:
                         weights = work.tile([P, K], BF16, name="weights")[:]
                     lang_block = lang_bf[:, :, i * P : (i + 1) * P]
-                    mixes.append(
-                        softmax_and_mix(
-                            STARTS[j] // P + i, lang_block, weights, j == len(PIECES) - 1, j >= len(PIECES) - 2
-                        )
-                    )
+                    mixes.append(softmax_and_mix(STARTS[j] // P + i, lang_block, weights, len(PIECES) - 1 - j))
                 j += 1
 
-        late_blocks = STARTS[-2] // P
-        nc.vector.reciprocal(inverses[:, :late_blocks], totals[:, :late_blocks])
-        divided = held.tile([P, late_blocks, D], F32, name="divided")
-        for i in range(late_blocks):
-            nc.vector.tensor_scalar_mul(divided[:, i, :], mixes[i], inverses[:, i : i + 1])
-        late_ident = lang_bf.rearrange("p b n -> p (b n)").bitcast(F32)
-        nc.vector.tensor_copy(late_ident, ident_f32[:])
+        last_block, early_blocks = STARTS[-1] // P, STARTS[-2] // P
+        divided = held.tile([P, last_block, D], F32, name="divided")
+        for blocks in (range(early_blocks), range(early_blocks, last_block)):
+            sharing = slice(blocks.start, blocks.stop)
+            nc.vector.reciprocal(inverses[:, sharing], totals[:, sharing])
+            for i in blocks:
+                nc.vector.tensor_scalar_mul(divided[:, i, :], mixes[i], inverses[:, i : i + 1])
         out_blocks = out.rearrange("(b p) n -> p b n", p=P)
-        for j in range(len(PIECES)):
-            words = slice(STARTS[j], STARTS[j] + PIECES[j])
-            if j < len(PIECES) - 2:
-                back = psum.tile([P, DB, PIECES[j]], F32, name="back")
-                for i in range(words.start // P, words.stop // P):
-                    columns = slice(i * P - words.start, (i + 1) * P - words.start)
-                    for b in range(DB):
-                        nc.tensor.transpose(back[:, b, columns], divided[:, i, b * P : (b + 1) * P], late_ident)
+        for i in range(W // P):
+            mix = mixes[i]
+            if i < last_block:
+                back = psum.tile([P, DB, P], F32, name="back")
+                for b in range(DB):
+                    nc.tensor.transpose(back[:, b, :], divided[:, i, b * P : (b + 1) * P], late_ident(lang_bf))
                 mix = back[:]
-            else:
-                mix = mixes[words.start // P]
+            words = slice(i * P, (i + 1) * P)
             nc.vector.tensor_tensor(result[:, :, words], mix, lang[:, :, words], ADD)
             nc.sync.dma_start(out_blocks[:, :, words], result[:, :, words])

@@ -13,11 +13,11 @@ D, S, T, W, K = 256, 4096, 8, 1024, 512
 DB = D // P
 KB = K // P
 GROUPS = ((256, 256), (256,), (128, 128))
+EARLY = (T - 2, T // 2, T // 2)
 PIECES = [width for group in GROUPS for width in group]
 assert sum(PIECES) == W
 STARTS = [sum(PIECES[:i]) for i in range(len(PIECES))]
 HALF = W // 2
-EARLY = T // 2
 SOFT = 8.0
 
 FLOPS = 4 * W * K * D
@@ -84,12 +84,16 @@ def tile_sde_kernel(tc, table, latent, offs, out):
             return running
 
         operands = held.tile([P, max(PIECES) // P, K], BF16, name="operands")
+        second_lang = held.tile([P, DB, PIECES[1]], BF16, name="second_lang")
 
-        def look_up(j, early):
+        def look_up(j, early, late_terms):
             width = PIECES[j]
             piece = slice(STARTS[j], STARTS[j] + width)
-            add_terms(range(EARLY, T), piece, early, lang[:, :, piece], late_sums)
-            lang_bf = operands[:, max(PIECES) // P - 1, : DB * width].rearrange("p (b n) -> p b n", b=DB)
+            add_terms(late_terms, piece, early, lang[:, :, piece], late_sums)
+            if j == 1:
+                lang_bf = second_lang[:]
+            else:
+                lang_bf = operands[:, max(PIECES) // P - 1, : DB * width].rearrange("p (b n) -> p b n", b=DB)
             for b in range(DB):
                 nc.scalar.activation(lang_bf[:, b, :], lang[:, b, piece], ACT.Tanh, scale=1.0 / T)
             nc.scalar.activation(lang[:, :, piece], lang[:, :, piece], ACT.Tanh, scale=1.0 / T)
@@ -161,16 +165,16 @@ def tile_sde_kernel(tc, table, latent, offs, out):
 
         mixes = []
         j = 0
-        for group in GROUPS:
+        for group, early_terms in zip(GROUPS, EARLY):
             start = STARTS[j]
             words = slice(start, start + sum(group))
             if start % HALF == 0:
                 first = first_terms(slice(start, start + HALF), early_sums if start == 0 else held)
             terms_before = first[:, :, start % HALF : start % HALF + sum(group)]
-            early = add_terms(range(1, EARLY), words, terms_before, None, early_sums)
+            early = add_terms(range(1, early_terms), words, terms_before, None, early_sums)
             for width in group:
                 piece_early = early[:, :, STARTS[j] - start : STARTS[j] - start + width]
-                lang_bf = look_up(j, piece_early)
+                lang_bf = look_up(j, piece_early, range(early_terms, T))
                 for i in range(width // P):
                     if j < len(PIECES) - 2:
                         weights = operands[:, i, :]
@@ -182,16 +186,16 @@ def tile_sde_kernel(tc, table, latent, offs, out):
 
         last_block, early_blocks = STARTS[-1] // P, STARTS[-2] // P
         divided = held.tile([P, last_block, D], F32, name="divided")
-        for blocks in (range(early_blocks), range(early_blocks, last_block)):
+        for blocks in (range(early_blocks, last_block), range(early_blocks)):
             sharing = slice(blocks.start, blocks.stop)
             nc.vector.reciprocal(inverses[:, sharing], totals[:, sharing])
             for i in blocks:
                 nc.vector.tensor_scalar_mul(divided[:, i, :], mixes[i], inverses[:, i : i + 1])
         out_blocks = out.rearrange("(b p) n -> p b n", p=P)
-        for i in range(W // P):
+        for i in (*range(early_blocks, W // P), *range(early_blocks)):
             mix = mixes[i]
             if i < last_block:
-                back = psum.tile([P, DB, P], F32, name="back")
+                back = psum.tile([P, DB, P], F32, name="back", tag="scores" if i == early_blocks else "back")
                 for b in range(DB):
                     nc.tensor.transpose(back[:, b, :], divided[:, i, b * P : (b + 1) * P], late_ident(lang_bf))
                 mix = back[:]

import math

import concourse.mybir as mybir
from concourse.masks import make_identity

F32, BF16, U16, U32 = mybir.dt.float32, mybir.dt.bfloat16, mybir.dt.uint16, mybir.dt.uint32
ADD = mybir.AluOpType.add
ACT = mybir.ActivationFunctionType
X = mybir.AxisListType.X

P = 128
D, S, T, W, K = 256, 4096, 8, 1024, 512
DB = D // P
KB = K // P
GROUPS = ((256, 256), (256,), (128, 128))
EARLY = (T - 2, T // 2, T // 2)
PIECES = [width for group in GROUPS for width in group]
assert sum(PIECES) == W
STARTS = [sum(PIECES[:i]) for i in range(len(PIECES))]
HALF = W // 2
SOFT = 8.0

FLOPS = 4 * W * K * D


def tile_sde_kernel(tc, table, latent, offs, out):
    nc = tc.nc
    with (
        tc.tile_pool(name="held", bufs=1) as held,
        tc.tile_pool(name="early", bufs=3) as early_sums,
        tc.tile_pool(name="late", bufs=4) as late_sums,
        tc.tile_pool(name="work", bufs=2) as work,
        tc.tile_pool(name="stats", bufs=4) as stats,
        tc.psum_pool(name="psum", bufs=2) as psum,
    ):
        offsets = held.tile([P, T * W // 16], U16, name="offsets")
        nc.sync.dma_start(offsets[:], offs)
        tables = [held.tile([P, S], F32, name=f"table{b}") for b in range(DB)]
        for b in range(DB):
            nc.sync.dma_start(tables[b][:], table[b * P : (b + 1) * P, :])
        codes = held.tile([P, KB, D], BF16, name="codes")
        nc.sync.dma_start(codes[:], latent.rearrange("(c p) d -> p c d", p=P))

        ident_bf = held.tile([P, P], BF16, name="ident_bf")
        make_identity(nc, ident_bf[:])
        ident_f32 = held.tile([P, P], F32, name="ident_f32")
        make_identity(nc, ident_f32[:])

        codesT = [held.tile([P, K], BF16, name=f"codesT{b}") for b in range(DB)]
        for b in range(DB):
            flipped = psum.tile([P, K], BF16, name="flipped")
            for c in range(KB):
                nc.tensor.transpose(
                    flipped[:, c * P : (c + 1) * P], codes[:, c, b * P : (b + 1) * P], ident_bf[:]
                )
            nc.scalar.copy(codesT[b][:], flipped[:])

        lang = held.tile([P, DB, W], F32, name="lang")
        mixed = held.tile([P, W // P, D], F32, name="mixed")
        totals = held.tile([P, W // P], F32, name="totals")
        inverses = held.tile([P, W // P], F32, name="inverses")
        result = held.tile([P, DB, W], F32, name="result")

        def first_terms(words, ring):
            width = words.stop - words.start
            first = ring.tile([P, DB, width], F32, name="partial")
            for b in range(DB):
                picked = tables[b][:].indirect(offsets[:, words.start // 16 : words.stop // 16])
                nc.vector.tensor_copy(first[:, b, :], picked)
            return first

        def add_terms(terms, words, running, last, ring):
            width = words.stop - words.start
            for t in terms:
                first_col = (t * W + words.start) // 16
                if last is None or t < terms[-1]:
                    partial = ring.tile([P, DB, width], F32, name="partial")[:]
                else:
                    partial = last
                for b in range(DB):
                    picked = tables[b][:].indirect(offsets[:, first_col : first_col + width // 16])
                    nc.vector.tensor_tensor(partial[:, b, :], picked, running[:, b, :], ADD)
                running = partial
            return running

        operands = held.tile([P, max(PIECES) // P, K], BF16, name="operands")
        second_lang = held.tile([P, DB, PIECES[1]], BF16, name="second_lang")

        def look_up(j, early, late_terms):
            width = PIECES[j]
            piece = slice(STARTS[j], STARTS[j] + width)
            add_terms(late_terms, piece, early, lang[:, :, piece], late_sums)
            if j == 1:
                lang_bf = second_lang[:]
            else:
                lang_bf = operands[:, max(PIECES) // P - 1, : DB * width].rearrange("p (b n) -> p b n", b=DB)
            for b in range(DB):
                nc.scalar.activation(lang_bf[:, b, :], lang[:, b, piece], ACT.Tanh, scale=1.0 / T)
            nc.scalar.activation(lang[:, :, piece], lang[:, :, piece], ACT.Tanh, scale=1.0 / T)
            return lang_bf

        def late_ident(lang_block):
            return lang_block.rearrange("p b n -> p (b n)").bitcast(F32)

        def softmax_and_mix(i, lang_block, weights, left):
            scores = psum.tile([P, K], F32, name="scores")
            for b in range(DB):
                nc.tensor.matmul(
                    scores[:], lang_block[:, b, :], codesT[b][:], start=(b == 0), stop=(b == DB - 1)
                )
            negshift = stats.tile([P, 1], F32, name="negshift")
            if left == 0:
                nc.vector.tensor_copy(late_ident(lang_block), ident_f32[:])
                nc.vector.reduce_max(negshift[:], scores[:], axis=X, negate=True)
            else:
                tempered = operands[:, max(PIECES) // P - 1, :] if left == 1 else work.tile([P, K], BF16, name="tempered")[:]
                tempered_sum = stats.tile([P, 1], F32, name="tempered_sum")
                nc.scalar.activation(
                    tempered, scores[:], ACT.Exp, scale=1.0 / SOFT, accum_out=tempered_sum[:]
                )
                nc.scalar.activation(
                    negshift[:],
                    tempered_sum[:].bitcast(U32),
                    ACT.Copy,
                    scale=-SOFT * math.log(2.0) / 2.0**23,
                    bias=SOFT * math.log(2.0) * 127.0,
                )
            if left == 0:
                exps = work.tile([P, K], F32, name="exps")
                nc.scalar.activation(
                    exps[:], scores[:], ACT.Exp, bias=negshift[:], accum_out=totals[:, i : i + 1]
                )
                nc.vector.reciprocal(inverses[:, i : i + 1], totals[:, i : i + 1])
                nc.vector.tensor_scalar_mul(weights, exps[:], inverses[:, i : i + 1])
            else:
                nc.scalar.activation(
                    weights, scores[:], ACT.Exp, bias=negshift[:], accum_out=totals[:, i : i + 1]
                )

            flipped = psum.tile([P, K], BF16, name="flipped")
            for c in range(KB):
                nc.tensor.transpose(
                    flipped[:, c * P : (c + 1) * P], weights[:, c * P : (c + 1) * P], ident_bf[:]
                )
            weightsT = work.tile([P, K], BF16, name="weightsT")
            nc.scalar.copy(weightsT[:], flipped[:])
            mix = psum.tile([P, D], F32, name="mix")
            if left == 0:
                for b in range(DB):
                    features = slice(b * P, (b + 1) * P)
                    for c in range(KB):
                        nc.tensor.matmul(
                            mix[:, features], codes[:, c, features], weightsT[:, c * P : (c + 1) * P],
                            start=(c == 0), stop=(c == KB - 1),
                        )
                return mix[:].rearrange("p (b n) -> p b n", b=DB)
            for c in range(KB):
                nc.tensor.matmul(
                    mix[:], weightsT[:, c * P : (c + 1) * P], codes[:, c, :], start=(c == 0), stop=(c == KB - 1)
                )
            if left == 1:
                return mix[:]
            nc.scalar.copy(mixed[:, i, :], mix[:])
            return mixed[:, i, :]

        mixes = []
        j = 0
        for group, early_terms in zip(GROUPS, EARLY):
            start = STARTS[j]
            words = slice(start, start + sum(group))
            if start % HALF == 0:
                first = first_terms(slice(start, start + HALF), early_sums if start == 0 else held)
            terms_before = first[:, :, start % HALF : start % HALF + sum(group)]
            early = add_terms(range(1, early_terms), words, terms_before, None, early_sums)
            for width in group:
                piece_early = early[:, :, STARTS[j] - start : STARTS[j] - start + width]
                lang_bf = look_up(j, piece_early, range(early_terms, T))
                for i in range(width // P):
                    if j < len(PIECES) - 2:
                        weights = operands[:, i, :]
                    else:
                        weights = work.tile([P, K], BF16, name="weights")[:]
                    lang_block = lang_bf[:, :, i * P : (i + 1) * P]
                    mixes.append(softmax_and_mix(STARTS[j] // P + i, lang_block, weights, len(PIECES) - 1 - j))
                j += 1

        last_block, early_blocks = STARTS[-1] // P, STARTS[-2] // P
        divided = held.tile([P, last_block, D], F32, name="divided")
        for blocks in (range(early_blocks, last_block), range(early_blocks)):
            sharing = slice(blocks.start, blocks.stop)
            nc.vector.reciprocal(inverses[:, sharing], totals[:, sharing])
            for i in blocks:
                nc.vector.tensor_scalar_mul(divided[:, i, :], mixes[i], inverses[:, i : i + 1])
        out_blocks = out.rearrange("(b p) n -> p b n", p=P)
        for i in (*range(early_blocks, W // P), *range(early_blocks)):
            mix = mixes[i]
            if i < last_block:
                back = psum.tile([P, DB, P], F32, name="back", tag="scores" if i == early_blocks else "back")
                for b in range(DB):
                    nc.tensor.transpose(back[:, b, :], divided[:, i, b * P : (b + 1) * P], late_ident(lang_bf))
                mix = back[:]
            words = slice(i * P, (i + 1) * P)
            nc.vector.tensor_tensor(result[:, :, words], mix, lang[:, :, words], ADD)
            nc.sync.dma_start(out_blocks[:, :, words], result[:, :, words])
